import numpy as np
import ml_dtypes


def mxq(x, axis, fmt="e4m3"):
    dtype, down = {"e4m3": (ml_dtypes.float8_e4m3fn, 7), "e5m2": (ml_dtypes.float8_e5m2, 14)}[fmt]
    v = np.moveaxis(np.asarray(x, np.float32).astype(ml_dtypes.bfloat16).astype(np.float64), axis, -1)
    blocks = v.reshape(v.shape[:-1] + (-1, 32))
    amax = np.abs(blocks).max(-1, keepdims=True)
    byte = np.maximum(np.where(amax > 0, np.frexp(amax)[1] - 1 + 127, 0) - down, 1)
    scale = np.exp2(byte - 127.0)
    codes = (blocks / scale).astype(np.float32).astype(dtype).astype(np.float64)
    return np.moveaxis((codes * scale).reshape(v.shape), -1, axis)


WIDE = False


def mx_kscale(k):
    if not WIDE:
        return np.ones(k)
    levels = np.array([20, -20, 10, -10, 0])
    a = np.random.permutation(np.resize(levels, k // 512 * 4)).reshape(k // 512, 4)
    idx = np.arange(k)
    return np.exp2(a[idx // 512, idx % 128 // 32])


BF16 = ml_dtypes.bfloat16


def bf(x):
    return np.asarray(x, np.float32).astype(BF16)


def f64(x):
    return np.asarray(x).astype(np.float64)


B, CIN, COUT, H, W = 2, 512, 512, 64, 64


def setup_inputs():
    u = mx_kscale(COUT)
    x = np.random.standard_normal((B, CIN, H, W))
    weight = np.random.uniform(-1.0, 1.0, (CIN, COUT)) * np.sqrt(3.0 / CIN) / u[None, :]
    g = np.random.standard_normal((B, COUT, H, W)) * np.exp2(np.random.randint(-12, 1, (B, 1, H, W))) * 4.0 * u[None, :, None, None]
    return {"x": bf(x), "weight": bf(weight), "grad_out": bf(g)}


def reference(x, weight, grad_out):
    wq = mxq(f64(weight), 1, "e4m3")
    gq = mxq(f64(grad_out), 1, "e5m2")
    return np.einsum("io,bohw->bihw", wq, gq, optimize=True)

@@ -1,0 +1,99 @@
+from contextlib import ExitStack
+
+import concourse.mybir as mybir
+from concourse.masks import make_identity
+
+BF16 = mybir.dt.bfloat16
+F32 = mybir.dt.float32
+U32 = mybir.dt.uint32
+U8 = mybir.dt.uint8
+E4X4 = mybir.dt.float8_e4m3fn_x4
+E5X4 = mybir.dt.float8_e5m2_x4
+
+P = 128
+PACK = 4
+B, CIN, COUT, HW = 2, 512, 512, 4096
+N_TILE = 512
+M_TILES = CIN // P
+STORE_PX = 2048
+
+FLOPS = 2 * B * HW * CIN * COUT
+BYTES = 2 * B * COUT * HW + 2 * CIN * COUT + 4 * B * CIN * HW
+
+LOADS = ((0, 0, 2048), (0, 2048, 2048), (1, 0, 4096))
+
+
+def tile_simpleconvolution_t_kernel(tc, x, weight, grad_out, out):
+    nc = tc.nc
+    with ExitStack() as ctx:
+        keep = ctx.enter_context(tc.tile_pool(name="keep", bufs=1))
+        stage = ctx.enter_context(tc.tile_pool(name="stage", bufs=3))
+        quant = ctx.enter_context(tc.tile_pool(name="quant", bufs=4))
+        outs = ctx.enter_context(tc.tile_pool(name="outs", bufs=12))
+        psum = ctx.enter_context(tc.psum_pool(name="psum", bufs=8))
+
+        w_raw = keep.tile([P, M_TILES, COUT], BF16, name="w_raw")
+        nc.sync.dma_start(out=w_raw[:], in_=weight.rearrange("(p t) k -> p t k", t=M_TILES))
+        g_raw = []
+        for n, (b, px0, npx) in enumerate(LOADS):
+            g = keep.tile([P, PACK, npx], BF16, name="g_raw%d" % n)
+            src = grad_out[b].rearrange("(p j) h w -> p j (h w)", j=PACK)
+            nc.sync.dma_start(out=g[:], in_=src[:, :, px0 : px0 + npx])
+            g_raw.append(g)
+
+        ident = keep.tile([P, P], F32, name="ident")
+        make_identity(nc, ident[:])
+        w_grouped = keep.tile([P, M_TILES * P * PACK], BF16, name="w_grouped", align_bytes=64)
+        w_codes = keep.tile([P, M_TILES * P], U32, name="w_codes", align_bytes=64)
+        w_scales = keep.tile([P, M_TILES * P], U8, name="w_scales", align_bytes=64)
+        w_words = w_raw[:].bitcast(F32).rearrange("p t (q u) -> p t u q", u=2)
+        w_grouped_words = w_grouped[:].bitcast(F32).rearrange("p (t i u) -> p t i u", t=M_TILES, u=2)
+        for half in range(2):
+            bank = psum.tile([P, N_TILE], F32, name="bank", tag="bank")
+            planes = bank[:].rearrange("p (t u i) -> p t u i", t=2, u=2)
+            for tt in range(2):
+                for u in range(2):
+                    nc.tensor.transpose(planes[:, tt, u, :], w_words[:, 2 * half + tt, u, :], ident[:])
+            nc.scalar.copy(
+                out=w_grouped_words[:, 2 * half : 2 * half + 2, :, :],
+                in_=planes.rearrange("p t u i -> p t i u"),
+            )
+        nc.vector.quantize_mx(out=w_codes[:].bitcast(E4X4), scales=w_scales[:], in_=w_grouped[:])
+
+        for n, (b, px0, npx) in enumerate(LOADS):
+            out_b = out[b].rearrange("(p t) h w -> p t (h w)", t=M_TILES)
+            for s0 in range(0, npx, STORE_PX):
+                o_tiles = []
+                for t in range(M_TILES):
+                    o = outs.tile([P, STORE_PX], F32, name="o", tag="o")
+                    o_tiles.append(o)
+                for c0 in range(0, STORE_PX, N_TILE):
+                    cols = slice(s0 + c0, s0 + c0 + N_TILE)
+                    grouped = stage.tile([P, N_TILE, PACK], BF16, name="grouped", tag="grouped", align_bytes=64)
+                    nc.vector.tensor_copy(
+                        out=grouped[:].rearrange("p (c i) j -> p c j i", i=4),
+                        in_=g_raw[n][:, :, cols].rearrange("p j (c i) -> p c j i", i=4),
+                    )
+                    codes = quant.tile([P, N_TILE], U32, name="codes", tag="codes", align_bytes=64)
+                    scales = quant.tile([P, N_TILE], U8, name="scales", tag="scales", align_bytes=64)
+                    nc.vector.quantize_mx(
+                        out=codes[:].bitcast(E5X4),
+                        scales=scales[:],
+                        in_=grouped[:].rearrange("p w j -> p (w j)"),
+                    )
+                    for t in range(M_TILES):
+                        acc = psum.tile([P, N_TILE], F32, name="acc", tag="bank")
+                        nc.tensor.matmul_mx(
+                            out=acc[:],
+                            lhsT=w_codes[:, t * P : (t + 1) * P].bitcast(E4X4),
+                            lhsT_scale=w_scales[:, t * P : (t + 1) * P],
+                            rhs=codes[:].bitcast(E5X4),
+                            rhs_scale=scales[:],
+                            start=True,
+                            stop=True,
+                        )
+                        nc.scalar.copy(out=o_tiles[t][:, c0 : c0 + N_TILE], in_=acc[:])
+                for t in range(M_TILES):
+                    nc.sync.dma_start(
+                        out=out_b[:, t, px0 + s0 : px0 + s0 + STORE_PX], in_=o_tiles[t][:]
+                    )

@@ -69,6 +69,7 @@ def tile_simpleconvolution_t_kernel(tc, x, weight, grad_out, out):
                     o_tiles.append(o)
                 for c0 in range(0, STORE_PX, N_TILE):
                     cols = slice(s0 + c0, s0 + c0 + N_TILE)
+                    odd_chunk = (c0 // N_TILE) % 2 == 1
                     grouped = stage.tile([P, N_TILE, PACK], BF16, name="grouped", tag="grouped", align_bytes=64)
                     nc.vector.tensor_copy(
                         out=grouped[:].rearrange("p (c i) j -> p c j i", i=4),
@@ -92,7 +93,10 @@ def tile_simpleconvolution_t_kernel(tc, x, weight, grad_out, out):
                             start=True,
                             stop=True,
                         )
-                        nc.scalar.copy(out=o_tiles[t][:, c0 : c0 + N_TILE], in_=acc[:])
+                        if odd_chunk and t == M_TILES - 1:
+                            nc.vector.tensor_copy(out=o_tiles[t][:, c0 : c0 + N_TILE], in_=acc[:])
+                        else:
+                            nc.scalar.copy(out=o_tiles[t][:, c0 : c0 + N_TILE], in_=acc[:])
                 for t in range(M_TILES):
                     nc.sync.dma_start(
                         out=out_b[:, t, px0 + s0 : px0 + s0 + STORE_PX], in_=o_tiles[t][:]

@@ -16,11 +16,12 @@ B, CIN, COUT, HW = 2, 512, 512, 4096
 N_TILE = 512
 M_TILES = CIN // P
 STORE_PX = 2048
+CHUNKS_PER_STORE = STORE_PX // N_TILE
 
 FLOPS = 2 * B * HW * CIN * COUT
 BYTES = 2 * B * COUT * HW + 2 * CIN * COUT + 4 * B * CIN * HW
 
-LOADS = ((0, 0, 2048), (0, 2048, 2048), (1, 0, 4096))
+LOADS = ((0, 0, 512), (0, 512, 512), (0, 1024, 1024), (0, 2048, 2048), (1, 0, 4096))
 
 
 def tile_simpleconvolution_t_kernel(tc, x, weight, grad_out, out):
@@ -41,6 +42,12 @@ def tile_simpleconvolution_t_kernel(tc, x, weight, grad_out, out):
             nc.sync.dma_start(out=g[:], in_=src[:, :, px0 : px0 + npx])
             g_raw.append(g)
 
+        def raw_chunk(b, px):
+            for n, (lb, px0, npx) in enumerate(LOADS):
+                if lb == b and px0 <= px < px0 + npx:
+                    return g_raw[n][:, :, px - px0 : px - px0 + N_TILE]
+            raise ValueError("no load holds this chunk")
+
         ident = keep.tile([P, P], F32, name="ident")
         make_identity(nc, ident[:])
         w_grouped = keep.tile([P, M_TILES * P * PACK], BF16, name="w_grouped", align_bytes=64)
@@ -58,46 +65,59 @@ def tile_simpleconvolution_t_kernel(tc, x, weight, grad_out, out):
                 out=w_grouped_words[:, 2 * half : 2 * half + 2, :, :],
                 in_=planes.rearrange("p t u i -> p t i u"),
             )
-        nc.vector.quantize_mx(out=w_codes[:].bitcast(E4X4), scales=w_scales[:], in_=w_grouped[:])
 
-        for n, (b, px0, npx) in enumerate(LOADS):
-            out_b = out[b].rearrange("(p t) h w -> p t (h w)", t=M_TILES)
-            for s0 in range(0, npx, STORE_PX):
+        chunks = [(b, px) for b in range(B) for px in range(0, HW, N_TILE)]
+
+        def regroup(c):
+            b, px = chunks[c]
+            grouped = stage.tile([P, N_TILE, PACK], BF16, name="grouped", tag="grouped", align_bytes=64)
+            nc.vector.tensor_copy(
+                out=grouped[:].rearrange("p (c i) j -> p c j i", i=4),
+                in_=raw_chunk(b, px).rearrange("p j (c i) -> p c j i", i=4),
+            )
+            return grouped
+
+        def quantise(grouped):
+            codes = quant.tile([P, N_TILE], U32, name="codes", tag="codes", align_bytes=64)
+            scales = quant.tile([P, N_TILE], U8, name="scales", tag="scales", align_bytes=64)
+            nc.vector.quantize_mx(
+                out=codes[:].bitcast(E5X4),
+                scales=scales[:],
+                in_=grouped[:].rearrange("p w j -> p (w j)"),
+            )
+            return codes, scales
+
+        grouped_next = regroup(0)
+        nc.vector.quantize_mx(out=w_codes[:].bitcast(E4X4), scales=w_scales[:], in_=w_grouped[:])
+        o_tiles = []
+        for c, (b, px) in enumerate(chunks):
+            grouped = grouped_next
+            if c + 1 < len(chunks):
+                grouped_next = regroup(c + 1)
+            codes, scales = quantise(grouped)
+            k = c % CHUNKS_PER_STORE
+            if k == 0:
                 o_tiles = []
                 for t in range(M_TILES):
                     o = outs.tile([P, STORE_PX], F32, name="o", tag="o")
                     o_tiles.append(o)
-                for c0 in range(0, STORE_PX, N_TILE):
-                    cols = slice(s0 + c0, s0 + c0 + N_TILE)
-                    odd_chunk = (c0 // N_TILE) % 2 == 1
-                    grouped = stage.tile([P, N_TILE, PACK], BF16, name="grouped", tag="grouped", align_bytes=64)
-                    nc.vector.tensor_copy(
-                        out=grouped[:].rearrange("p (c i) j -> p c j i", i=4),
-                        in_=g_raw[n][:, :, cols].rearrange("p j (c i) -> p c j i", i=4),
-                    )
-                    codes = quant.tile([P, N_TILE], U32, name="codes", tag="codes", align_bytes=64)
-                    scales = quant.tile([P, N_TILE], U8, name="scales", tag="scales", align_bytes=64)
-                    nc.vector.quantize_mx(
-                        out=codes[:].bitcast(E5X4),
-                        scales=scales[:],
-                        in_=grouped[:].rearrange("p w j -> p (w j)"),
-                    )
-                    for t in range(M_TILES):
-                        acc = psum.tile([P, N_TILE], F32, name="acc", tag="bank")
-                        nc.tensor.matmul_mx(
-                            out=acc[:],
-                            lhsT=w_codes[:, t * P : (t + 1) * P].bitcast(E4X4),
-                            lhsT_scale=w_scales[:, t * P : (t + 1) * P],
-                            rhs=codes[:].bitcast(E5X4),
-                            rhs_scale=scales[:],
-                            start=True,
-                            stop=True,
-                        )
-                        if odd_chunk and t == M_TILES - 1:
-                            nc.vector.tensor_copy(out=o_tiles[t][:, c0 : c0 + N_TILE], in_=acc[:])
-                        else:
-                            nc.scalar.copy(out=o_tiles[t][:, c0 : c0 + N_TILE], in_=acc[:])
-                for t in range(M_TILES):
-                    nc.sync.dma_start(
-                        out=out_b[:, t, px0 + s0 : px0 + s0 + STORE_PX], in_=o_tiles[t][:]
-                    )
+            for t in range(M_TILES):
+                acc = psum.tile([P, N_TILE], F32, name="acc", tag="bank")
+                nc.tensor.matmul_mx(
+                    out=acc[:],
+                    lhsT=w_codes[:, t * P : (t + 1) * P].bitcast(E4X4),
+                    lhsT_scale=w_scales[:, t * P : (t + 1) * P],
+                    rhs=codes[:].bitcast(E5X4),
+                    rhs_scale=scales[:],
+                    start=True,
+                    stop=True,
+                )
+                dst = o_tiles[t][:, k * N_TILE : (k + 1) * N_TILE]
+                if c % 2 == 1 and t == M_TILES - 1:
+                    nc.vector.tensor_copy(out=dst, in_=acc[:])
+                else:
+                    nc.scalar.copy(out=dst, in_=acc[:])
+                if k == CHUNKS_PER_STORE - 1:
+                    out_b = out[b].rearrange("(p t) h w -> p t (h w)", t=M_TILES)
+                    first = px + N_TILE - STORE_PX
+                    nc.sync.dma_start(out=out_b[:, t, first : first + STORE_PX], in_=o_tiles[t][:])

@@ -21,7 +21,8 @@ CHUNKS_PER_STORE = STORE_PX // N_TILE
 FLOPS = 2 * B * HW * CIN * COUT
 BYTES = 2 * B * COUT * HW + 2 * CIN * COUT + 4 * B * CIN * HW
 
-LOADS = ((0, 0, 512), (0, 512, 512), (0, 1024, 1024), (0, 2048, 2048), (1, 0, 4096))
+LOADS = ((0, 0, 1536), (0, 1536, 2560), (1, 0, 4096))
+EARLY_QUANT = ()
 
 
 def tile_simpleconvolution_t_kernel(tc, x, weight, grad_out, out):
@@ -32,6 +33,7 @@ def tile_simpleconvolution_t_kernel(tc, x, weight, grad_out, out):
         quant = ctx.enter_context(tc.tile_pool(name="quant", bufs=4))
         outs = ctx.enter_context(tc.tile_pool(name="outs", bufs=12))
         psum = ctx.enter_context(tc.psum_pool(name="psum", bufs=8))
+        ctx.enter_context(tc.manual_schedule())
 
         w_raw = keep.tile([P, M_TILES, COUT], BF16, name="w_raw")
         nc.sync.dma_start(out=w_raw[:], in_=weight.rearrange("(p t) k -> p t k", t=M_TILES))
@@ -67,6 +69,11 @@ def tile_simpleconvolution_t_kernel(tc, x, weight, grad_out, out):
             )
 
         chunks = [(b, px) for b in range(B) for px in range(0, HW, N_TILE)]
+        last = len(chunks) - 1
+        grouped_of = {}
+        o_tiles = {}
+        late = []
+        done = {"late": 0}
 
         def regroup(c):
             b, px = chunks[c]
@@ -75,33 +82,39 @@ def tile_simpleconvolution_t_kernel(tc, x, weight, grad_out, out):
                 out=grouped[:].rearrange("p (c i) j -> p c j i", i=4),
                 in_=raw_chunk(b, px).rearrange("p j (c i) -> p c j i", i=4),
             )
-            return grouped
+            grouped_of[c] = grouped
 
-        def quantise(grouped):
+        def quantise(c):
             codes = quant.tile([P, N_TILE], U32, name="codes", tag="codes", align_bytes=64)
             scales = quant.tile([P, N_TILE], U8, name="scales", tag="scales", align_bytes=64)
             nc.vector.quantize_mx(
                 out=codes[:].bitcast(E5X4),
                 scales=scales[:],
-                in_=grouped[:].rearrange("p w j -> p (w j)"),
+                in_=grouped_of[c][:].rearrange("p w j -> p (w j)"),
             )
             return codes, scales
 
-        grouped_next = regroup(0)
-        nc.vector.quantize_mx(out=w_codes[:].bitcast(E4X4), scales=w_scales[:], in_=w_grouped[:])
-        o_tiles = []
-        for c, (b, px) in enumerate(chunks):
-            grouped = grouped_next
-            if c + 1 < len(chunks):
-                grouped_next = regroup(c + 1)
-            codes, scales = quantise(grouped)
+        def store_if_full(c, t):
+            if c % CHUNKS_PER_STORE == CHUNKS_PER_STORE - 1:
+                b, px = chunks[c]
+                out_b = out[b].rearrange("(p t) h w -> p t (h w)", t=M_TILES)
+                first = px + N_TILE - STORE_PX
+                nc.sync.dma_start(
+                    out=out_b[:, t, first : first + STORE_PX], in_=o_tiles[(c // CHUNKS_PER_STORE, t)][:]
+                )
+
+        def vector_copies_out():
+            for c, t, acc, dst in late[done["late"] :]:
+                nc.vector.tensor_copy(out=dst, in_=acc[:])
+                store_if_full(c, t)
+            done["late"] = len(late)
+
+        def multiply(c, codes, scales):
             k = c % CHUNKS_PER_STORE
-            if k == 0:
-                o_tiles = []
-                for t in range(M_TILES):
-                    o = outs.tile([P, STORE_PX], F32, name="o", tag="o")
-                    o_tiles.append(o)
             for t in range(M_TILES):
+                if k == 0:
+                    o = outs.tile([P, STORE_PX], F32, name="o", tag="o")
+                    o_tiles[(c // CHUNKS_PER_STORE, t)] = o
                 acc = psum.tile([P, N_TILE], F32, name="acc", tag="bank")
                 nc.tensor.matmul_mx(
                     out=acc[:],
@@ -112,12 +125,24 @@ def tile_simpleconvolution_t_kernel(tc, x, weight, grad_out, out):
                     start=True,
                     stop=True,
                 )
-                dst = o_tiles[t][:, k * N_TILE : (k + 1) * N_TILE]
+                dst = o_tiles[(c // CHUNKS_PER_STORE, t)][:, k * N_TILE : (k + 1) * N_TILE]
                 if c % 2 == 1 and t == M_TILES - 1:
-                    nc.vector.tensor_copy(out=dst, in_=acc[:])
+                    late.append((c, t, acc, dst))
                 else:
                     nc.scalar.copy(out=dst, in_=acc[:])
-                if k == CHUNKS_PER_STORE - 1:
-                    out_b = out[b].rearrange("(p t) h w -> p t (h w)", t=M_TILES)
-                    first = px + N_TILE - STORE_PX
-                    nc.sync.dma_start(out=out_b[:, t, first : first + STORE_PX], in_=o_tiles[t][:])
+                    store_if_full(c, t)
+
+        regroup(0)
+        nc.vector.quantize_mx(out=w_codes[:].bitcast(E4X4), scales=w_scales[:], in_=w_grouped[:])
+        for c in range(len(chunks)):
+            if c in EARLY_QUANT or c == 0:
+                codes, scales = quantise(c)
+                if c < last:
+                    regroup(c + 1)
+            else:
+                if c < last:
+                    regroup(c + 1)
+                codes, scales = quantise(c)
+            vector_copies_out()
+            multiply(c, codes, scales)
+        vector_copies_out()

@@ -33,7 +33,6 @@ def tile_simpleconvolution_t_kernel(tc, x, weight, grad_out, out):
         quant = ctx.enter_context(tc.tile_pool(name="quant", bufs=4))
         outs = ctx.enter_context(tc.tile_pool(name="outs", bufs=12))
         psum = ctx.enter_context(tc.psum_pool(name="psum", bufs=8))
-        ctx.enter_context(tc.manual_schedule())
 
         w_raw = keep.tile([P, M_TILES, COUT], BF16, name="w_raw")
         nc.sync.dma_start(out=w_raw[:], in_=weight.rearrange("(p t) k -> p t k", t=M_TILES))

@@ -31,8 +31,9 @@ def tile_simpleconvolution_t_kernel(tc, x, weight, grad_out, out):
         keep = ctx.enter_context(tc.tile_pool(name="keep", bufs=1))
         stage = ctx.enter_context(tc.tile_pool(name="stage", bufs=3))
         quant = ctx.enter_context(tc.tile_pool(name="quant", bufs=4))
-        outs = ctx.enter_context(tc.tile_pool(name="outs", bufs=12))
+        outs = ctx.enter_context(tc.tile_pool(name="outs", bufs=6))
         psum = ctx.enter_context(tc.psum_pool(name="psum", bufs=8))
+        ctx.enter_context(tc.manual_schedule())
 
         w_raw = keep.tile([P, M_TILES, COUT], BF16, name="w_raw")
         nc.sync.dma_start(out=w_raw[:], in_=weight.rearrange("(p t) k -> p t k", t=M_TILES))
@@ -98,9 +99,11 @@ def tile_simpleconvolution_t_kernel(tc, x, weight, grad_out, out):
                 b, px = chunks[c]
                 out_b = out[b].rearrange("(p t) h w -> p t (h w)", t=M_TILES)
                 first = px + N_TILE - STORE_PX
-                nc.sync.dma_start(
-                    out=out_b[:, t, first : first + STORE_PX], in_=o_tiles[(c // CHUNKS_PER_STORE, t)][:]
-                )
+                if t % 2 == 1:
+                    nc.sync.dma_start(
+                        out=out_b[:, t - 1 : t + 1, first : first + STORE_PX],
+                        in_=o_tiles[(c // CHUNKS_PER_STORE, t // 2)][:],
+                    )
 
         def vector_copies_out():
             for c, t, acc, dst in late[done["late"] :]:
@@ -111,9 +114,9 @@ def tile_simpleconvolution_t_kernel(tc, x, weight, grad_out, out):
         def multiply(c, codes, scales):
             k = c % CHUNKS_PER_STORE
             for t in range(M_TILES):
-                if k == 0:
-                    o = outs.tile([P, STORE_PX], F32, name="o", tag="o")
-                    o_tiles[(c // CHUNKS_PER_STORE, t)] = o
+                if k == 0 and t % 2 == 0:
+                    o = outs.tile([P, 2, STORE_PX], F32, name="o", tag="o")
+                    o_tiles[(c // CHUNKS_PER_STORE, t // 2)] = o
                 acc = psum.tile([P, N_TILE], F32, name="acc", tag="bank")
                 nc.tensor.matmul_mx(
                     out=acc[:],
@@ -124,7 +127,7 @@ def tile_simpleconvolution_t_kernel(tc, x, weight, grad_out, out):
                     start=True,
                     stop=True,
                 )
-                dst = o_tiles[(c // CHUNKS_PER_STORE, t)][:, k * N_TILE : (k + 1) * N_TILE]
+                dst = o_tiles[(c // CHUNKS_PER_STORE, t // 2)][:, t % 2, k * N_TILE : (k + 1) * N_TILE]
                 if c % 2 == 1 and t == M_TILES - 1:
                     late.append((c, t, acc, dst))
                 else:

@@ -56,7 +56,7 @@ def tile_simpleconvolution_t_kernel(tc, x, weight, grad_out, out):
         w_codes = keep.tile([P, M_TILES * P], U32, name="w_codes", align_bytes=64)
         w_scales = keep.tile([P, M_TILES * P], U8, name="w_scales", align_bytes=64)
         w_words = w_raw[:].bitcast(F32).rearrange("p t (q u) -> p t u q", u=2)
-        w_grouped_words = w_grouped[:].bitcast(F32).rearrange("p (t i u) -> p t i u", t=M_TILES, u=2)
+        w_grouped_words = w_grouped[:].bitcast(F32).rearrange("p (i t u) -> p t i u", t=M_TILES, u=2)
         for half in range(2):
             bank = psum.tile([P, N_TILE], F32, name="bank", tag="bank")
             planes = bank[:].rearrange("p (t u i) -> p t u i", t=2, u=2)
@@ -97,7 +97,7 @@ def tile_simpleconvolution_t_kernel(tc, x, weight, grad_out, out):
         def store_if_full(c, t):
             if c % CHUNKS_PER_STORE == CHUNKS_PER_STORE - 1:
                 b, px = chunks[c]
-                out_b = out[b].rearrange("(p t) h w -> p t (h w)", t=M_TILES)
+                out_b = out[b].rearrange("(t p) h w -> p t (h w)", t=M_TILES)
                 first = px + N_TILE - STORE_PX
                 if t % 2 == 1:
                     nc.sync.dma_start(

@@ -15,43 +15,114 @@ PACK = 4
 B, CIN, COUT, HW = 2, 512, 512, 4096
 N_TILE = 512
 M_TILES = CIN // P
-STORE_PX = 2048
-CHUNKS_PER_STORE = STORE_PX // N_TILE
+GROUP = 4
+STORE_PX = GROUP * N_TILE
+CHUNKS = B * HW // N_TILE
+BATCH_CHUNKS = HW // N_TILE
 
 FLOPS = 2 * B * HW * CIN * COUT
 BYTES = 2 * B * COUT * HW + 2 * CIN * COUT + 4 * B * CIN * HW
 
-LOADS = ((0, 0, 1536), (0, 1536, 2560), (1, 0, 4096))
-EARLY_QUANT = ()
+LO_VECTOR = (0, 1, 2, 3)
+LO_SCALAR = (5, 6)
+HI_SCALAR = (2, 3)
+HI_LOADS = ((0, 4096),)
+V_BANKS = (
+    ((), (3,), (), ()),
+    ((), (3,), (), (3,)),
+    ((), (3,), (), (3,)),
+    ((1, 3), (1, 3), (1, 3), (1, 3)),
+)
 
 
 def tile_simpleconvolution_t_kernel(tc, x, weight, grad_out, out):
     nc = tc.nc
     with ExitStack() as ctx:
         keep = ctx.enter_context(tc.tile_pool(name="keep", bufs=1))
-        stage = ctx.enter_context(tc.tile_pool(name="stage", bufs=3))
-        quant = ctx.enter_context(tc.tile_pool(name="quant", bufs=4))
-        outs = ctx.enter_context(tc.tile_pool(name="outs", bufs=6))
+        stage = ctx.enter_context(tc.tile_pool(name="stage", bufs=8))
+        quant = ctx.enter_context(tc.tile_pool(name="quant", bufs=8))
+        outs = ctx.enter_context(tc.tile_pool(name="outs", bufs=12))
         psum = ctx.enter_context(tc.psum_pool(name="psum", bufs=8))
         ctx.enter_context(tc.manual_schedule())
 
         w_raw = keep.tile([P, M_TILES, COUT], BF16, name="w_raw")
+        b0_raw = keep.tile([P, PACK, HW], BF16, name="b0_raw")
+        b1_raw = keep.tile([P, PACK, HW], BF16, name="b1_raw")
+        raw = (b0_raw, b1_raw)
+        src0 = grad_out[0].rearrange("(p j) h w -> p j (h w)", j=PACK)
+        src1 = grad_out[1].rearrange("(p j) h w -> p j (h w)", j=PACK)
         nc.sync.dma_start(out=w_raw[:], in_=weight.rearrange("(p t) k -> p t k", t=M_TILES))
-        g_raw = []
-        for n, (b, px0, npx) in enumerate(LOADS):
-            g = keep.tile([P, PACK, npx], BF16, name="g_raw%d" % n)
-            src = grad_out[b].rearrange("(p j) h w -> p j (h w)", j=PACK)
-            nc.sync.dma_start(out=g[:], in_=src[:, :, px0 : px0 + npx])
-            g_raw.append(g)
-
-        def raw_chunk(b, px):
-            for n, (lb, px0, npx) in enumerate(LOADS):
-                if lb == b and px0 <= px < px0 + npx:
-                    return g_raw[n][:, :, px - px0 : px - px0 + N_TILE]
-            raise ValueError("no load holds this chunk")
+        nc.sync.dma_start(out=b0_raw[:, 0:2, :], in_=src0[:, 0:2, :])
+        for px0, npx in HI_LOADS:
+            nc.sync.dma_start(out=b0_raw[:, 2:4, px0 : px0 + npx], in_=src0[:, 2:4, px0 : px0 + npx])
+        nc.sync.dma_start(out=b1_raw[:], in_=src1)
 
         ident = keep.tile([P, P], F32, name="ident")
         make_identity(nc, ident[:])
+
+        grouped_of = {}
+        codes_of = {}
+        late = []
+
+        def regroup(c, j0, j1, on_scalar):
+            if c not in grouped_of:
+                grouped = stage.tile([P, N_TILE, PACK], BF16, name="grouped", tag="grouped", align_bytes=64)
+                grouped_of[c] = grouped
+            b, k = divmod(c, BATCH_CHUNKS)
+            dst = grouped_of[c][:].rearrange("p (c i) j -> p c j i", i=4)[:, :, j0:j1, :]
+            src = raw[b][:, j0:j1, k * N_TILE : (k + 1) * N_TILE].rearrange("p j (c i) -> p c j i", i=4)
+            if on_scalar:
+                nc.scalar.copy(out=dst, in_=src)
+            else:
+                nc.vector.tensor_copy(out=dst, in_=src)
+
+        def prepare(c):
+            if c in LO_VECTOR or c in LO_SCALAR:
+                regroup(c, 2, PACK, c in HI_SCALAR)
+            else:
+                regroup(c, 0, PACK, False)
+
+        def quantise(c):
+            codes = quant.tile([P, N_TILE], U32, name="codes", tag="codes", align_bytes=64)
+            scales = quant.tile([P, N_TILE], U8, name="scales", tag="scales", align_bytes=64)
+            nc.vector.quantize_mx(
+                out=codes[:].bitcast(E5X4),
+                scales=scales[:],
+                in_=grouped_of[c][:].rearrange("p w j -> p (w j)"),
+            )
+            codes_of[c] = (codes, scales)
+
+        def sweep(g, t):
+            o = outs.tile([P, STORE_PX], F32, name="o", tag="o")
+            for k in range(GROUP):
+                codes, scales = codes_of[g * GROUP + k]
+                acc = psum.tile([P, N_TILE], F32, name="acc", tag="bank")
+                nc.tensor.matmul_mx(
+                    out=acc[:],
+                    lhsT=w_codes[:, t * P : (t + 1) * P].bitcast(E4X4),
+                    lhsT_scale=w_scales[:, t * P : (t + 1) * P],
+                    rhs=codes[:].bitcast(E5X4),
+                    rhs_scale=scales[:],
+                    start=True,
+                    stop=True,
+                )
+                dst = o[:, k * N_TILE : (k + 1) * N_TILE]
+                if k in V_BANKS[g][t]:
+                    late.append((dst, acc))
+                else:
+                    nc.scalar.copy(out=dst, in_=acc[:])
+            return o
+
+        def vector_copies_out():
+            for dst, acc in late:
+                nc.vector.tensor_copy(out=dst, in_=acc[:])
+            late.clear()
+
+        def store(g, t, o):
+            b, px = divmod(g * STORE_PX, HW)
+            out_b = out[b].rearrange("(t p) h w -> t p (h w)", t=M_TILES)
+            nc.sync.dma_start(out=out_b[t, :, px : px + STORE_PX], in_=o[:])
+
         w_grouped = keep.tile([P, M_TILES * P * PACK], BF16, name="w_grouped", align_bytes=64)
         w_codes = keep.tile([P, M_TILES * P], U32, name="w_codes", align_bytes=64)
         w_scales = keep.tile([P, M_TILES * P], U8, name="w_scales", align_bytes=64)
@@ -68,83 +139,29 @@ def tile_simpleconvolution_t_kernel(tc, x, weight, grad_out, out):
                 in_=planes.rearrange("p t u i -> p t i u"),
             )
 
-        chunks = [(b, px) for b in range(B) for px in range(0, HW, N_TILE)]
-        last = len(chunks) - 1
-        grouped_of = {}
-        o_tiles = {}
-        late = []
-        done = {"late": 0}
+        for c in LO_SCALAR:
+            regroup(c, 0, 2, True)
+        for c in LO_VECTOR:
+            regroup(c, 0, 2, False)
+            if c == 0:
+                nc.vector.quantize_mx(out=w_codes[:].bitcast(E4X4), scales=w_scales[:], in_=w_grouped[:])
 
-        def regroup(c):
-            b, px = chunks[c]
-            grouped = stage.tile([P, N_TILE, PACK], BF16, name="grouped", tag="grouped", align_bytes=64)
-            nc.vector.tensor_copy(
-                out=grouped[:].rearrange("p (c i) j -> p c j i", i=4),
-                in_=raw_chunk(b, px).rearrange("p j (c i) -> p c j i", i=4),
-            )
-            grouped_of[c] = grouped
-
-        def quantise(c):
-            codes = quant.tile([P, N_TILE], U32, name="codes", tag="codes", align_bytes=64)
-            scales = quant.tile([P, N_TILE], U8, name="scales", tag="scales", align_bytes=64)
-            nc.vector.quantize_mx(
-                out=codes[:].bitcast(E5X4),
-                scales=scales[:],
-                in_=grouped_of[c][:].rearrange("p w j -> p (w j)"),
-            )
-            return codes, scales
-
-        def store_if_full(c, t):
-            if c % CHUNKS_PER_STORE == CHUNKS_PER_STORE - 1:
-                b, px = chunks[c]
-                out_b = out[b].rearrange("(t p) h w -> p t (h w)", t=M_TILES)
-                first = px + N_TILE - STORE_PX
-                if t % 2 == 1:
-                    nc.sync.dma_start(
-                        out=out_b[:, t - 1 : t + 1, first : first + STORE_PX],
-                        in_=o_tiles[(c // CHUNKS_PER_STORE, t // 2)][:],
-                    )
-
-        def vector_copies_out():
-            for c, t, acc, dst in late[done["late"] :]:
-                nc.vector.tensor_copy(out=dst, in_=acc[:])
-                store_if_full(c, t)
-            done["late"] = len(late)
-
-        def multiply(c, codes, scales):
-            k = c % CHUNKS_PER_STORE
+        for c in HI_SCALAR:
+            prepare(c)
+        prepare(0)
+        prepare(1)
+        for c in range(GROUP):
+            if c > 1 and c not in HI_SCALAR:
+                prepare(c)
+            quantise(c)
+        prepare(GROUP)
+        for g in range(CHUNKS // GROUP):
             for t in range(M_TILES):
-                if k == 0 and t % 2 == 0:
-                    o = outs.tile([P, 2, STORE_PX], F32, name="o", tag="o")
-                    o_tiles[(c // CHUNKS_PER_STORE, t // 2)] = o
-                acc = psum.tile([P, N_TILE], F32, name="acc", tag="bank")
-                nc.tensor.matmul_mx(
-                    out=acc[:],
-                    lhsT=w_codes[:, t * P : (t + 1) * P].bitcast(E4X4),
-                    lhsT_scale=w_scales[:, t * P : (t + 1) * P],
-                    rhs=codes[:].bitcast(E5X4),
-                    rhs_scale=scales[:],
-                    start=True,
-                    stop=True,
-                )
-                dst = o_tiles[(c // CHUNKS_PER_STORE, t // 2)][:, t % 2, k * N_TILE : (k + 1) * N_TILE]
-                if c % 2 == 1 and t == M_TILES - 1:
-                    late.append((c, t, acc, dst))
-                else:
-                    nc.scalar.copy(out=dst, in_=acc[:])
-                    store_if_full(c, t)
-
-        regroup(0)
-        nc.vector.quantize_mx(out=w_codes[:].bitcast(E4X4), scales=w_scales[:], in_=w_grouped[:])
-        for c in range(len(chunks)):
-            if c in EARLY_QUANT or c == 0:
-                codes, scales = quantise(c)
-                if c < last:
-                    regroup(c + 1)
-            else:
-                if c < last:
-                    regroup(c + 1)
-                codes, scales = quantise(c)
-            vector_copies_out()
-            multiply(c, codes, scales)
-        vector_copies_out()
+                o = sweep(g, t)
+                c = (g + 1) * GROUP + t
+                if c + 1 < CHUNKS:
+                    prepare(c + 1)
+                vector_copies_out()
+                if c < CHUNKS:
+                    quantise(c)
+                store(g, t, o)

@@ -15,21 +15,21 @@ PACK = 4
 B, CIN, COUT, HW = 2, 512, 512, 4096
 N_TILE = 512
 M_TILES = CIN // P
-GROUP = 4
-STORE_PX = GROUP * N_TILE
 CHUNKS = B * HW // N_TILE
 BATCH_CHUNKS = HW // N_TILE
 
 FLOPS = 2 * B * HW * CIN * COUT
 BYTES = 2 * B * COUT * HW + 2 * CIN * COUT + 4 * B * CIN * HW
 
-LO_VECTOR = (0, 1, 2, 3)
+LO_VECTOR = (0, 1, 2, 3, 4)
 LO_SCALAR = (5, 6)
-HI_SCALAR = (2, 3)
+HI_SCALAR = (1, 2)
 HI_LOADS = ((0, 4096),)
+GROUPS = (2, 3, 3, 4, 4)
 V_BANKS = (
-    ((), (3,), (), ()),
-    ((), (3,), (), (3,)),
+    ((), (), (), ()),
+    ((), (2,), (), ()),
+    ((), (2,), (), (2,)),
     ((), (3,), (), (3,)),
     ((1, 3), (1, 3), (1, 3), (1, 3)),
 )
@@ -93,9 +93,10 @@ def tile_simpleconvolution_t_kernel(tc, x, weight, grad_out, out):
             codes_of[c] = (codes, scales)
 
         def sweep(g, t):
-            o = outs.tile([P, STORE_PX], F32, name="o", tag="o")
-            for k in range(GROUP):
-                codes, scales = codes_of[g * GROUP + k]
+            first = sum(GROUPS[:g])
+            o = outs.tile([P, GROUPS[g] * N_TILE], F32, name="o", tag="o")
+            for k in range(GROUPS[g]):
+                codes, scales = codes_of[first + k]
                 acc = psum.tile([P, N_TILE], F32, name="acc", tag="bank")
                 nc.tensor.matmul_mx(
                     out=acc[:],
@@ -119,15 +120,15 @@ def tile_simpleconvolution_t_kernel(tc, x, weight, grad_out, out):
             late.clear()
 
         def store(g, t, o):
-            b, px = divmod(g * STORE_PX, HW)
-            out_b = out[b].rearrange("(t p) h w -> t p (h w)", t=M_TILES)
-            nc.sync.dma_start(out=out_b[t, :, px : px + STORE_PX], in_=o[:])
+            b, px = divmod(sum(GROUPS[:g]) * N_TILE, HW)
+            out_b = out[b].rearrange("(p t) h w -> t p (h w)", t=M_TILES)
+            nc.sync.dma_start(out=out_b[t, :, px : px + GROUPS[g] * N_TILE], in_=o[:])
 
         w_grouped = keep.tile([P, M_TILES * P * PACK], BF16, name="w_grouped", align_bytes=64)
         w_codes = keep.tile([P, M_TILES * P], U32, name="w_codes", align_bytes=64)
         w_scales = keep.tile([P, M_TILES * P], U8, name="w_scales", align_bytes=64)
         w_words = w_raw[:].bitcast(F32).rearrange("p t (q u) -> p t u q", u=2)
-        w_grouped_words = w_grouped[:].bitcast(F32).rearrange("p (i t u) -> p t i u", t=M_TILES, u=2)
+        w_grouped_words = w_grouped[:].bitcast(F32).rearrange("p (t i u) -> p t i u", t=M_TILES, u=2)
         for half in range(2):
             bank = psum.tile([P, N_TILE], F32, name="bank", tag="bank")
             planes = bank[:].rearrange("p (t u i) -> p t u i", t=2, u=2)
@@ -138,30 +139,37 @@ def tile_simpleconvolution_t_kernel(tc, x, weight, grad_out, out):
                 out=w_grouped_words[:, 2 * half : 2 * half + 2, :, :],
                 in_=planes.rearrange("p t u i -> p t i u"),
             )
+        nc.vector.quantize_mx(out=w_codes[:].bitcast(E4X4), scales=w_scales[:], in_=w_grouped[:])
 
         for c in LO_SCALAR:
             regroup(c, 0, 2, True)
         for c in LO_VECTOR:
             regroup(c, 0, 2, False)
-            if c == 0:
-                nc.vector.quantize_mx(out=w_codes[:].bitcast(E4X4), scales=w_scales[:], in_=w_grouped[:])
-
         for c in HI_SCALAR:
             prepare(c)
-        prepare(0)
-        prepare(1)
-        for c in range(GROUP):
-            if c > 1 and c not in HI_SCALAR:
-                prepare(c)
-            quantise(c)
-        prepare(GROUP)
-        for g in range(CHUNKS // GROUP):
+
+        done = {"prepared": 0, "quantised": 0}
+
+        def prepare_to(c):
+            while done["prepared"] < min(c, CHUNKS):
+                if done["prepared"] not in HI_SCALAR:
+                    prepare(done["prepared"])
+                done["prepared"] += 1
+
+        def quantise_to(c):
+            while done["quantised"] < c:
+                prepare_to(done["quantised"] + 2)
+                vector_copies_out()
+                quantise(done["quantised"])
+                done["quantised"] += 1
+
+        quantise_to(GROUPS[0])
+        for g in range(len(GROUPS)):
             for t in range(M_TILES):
                 o = sweep(g, t)
-                c = (g + 1) * GROUP + t
-                if c + 1 < CHUNKS:
-                    prepare(c + 1)
+                ahead = 0
+                if g + 1 < len(GROUPS):
+                    ahead = -(-(t + 1) * GROUPS[g + 1] // M_TILES)
+                quantise_to(sum(GROUPS[: g + 1]) + ahead)
                 vector_copies_out()
-                if c < CHUNKS:
-                    quantise(c)
                 store(g, t, o)

@@ -25,11 +25,11 @@ LO_VECTOR = (0, 1, 2, 3, 4)
 LO_SCALAR = (5, 6)
 HI_SCALAR = (1, 2)
 HI_LOADS = ((0, 4096),)
-GROUPS = (2, 3, 3, 4, 4)
+GROUPS = (2, 2, 4, 4, 4)
 V_BANKS = (
     ((), (), (), ()),
-    ((), (2,), (), ()),
-    ((), (2,), (), (2,)),
+    ((), (1,), (), ()),
+    ((), (3,), (), (3,)),
     ((), (3,), (), (3,)),
     ((1, 3), (1, 3), (1, 3), (1, 3)),
 )

@@ -23,12 +23,12 @@ BYTES = 2 * B * COUT * HW + 2 * CIN * COUT + 4 * B * CIN * HW
 
 LO_VECTOR = (0, 1, 2, 3, 4)
 LO_SCALAR = (5, 6)
-HI_SCALAR = (1, 2)
+HI_SCALAR = (2, 3)
 HI_LOADS = ((0, 4096),)
-GROUPS = (2, 2, 4, 4, 4)
+GROUP = 4
+AHEAD = ((0, 1, 2, 4), (1, 2, 3, 4), (1, 2, 3, 4), (0, 0, 0, 0))
 V_BANKS = (
-    ((), (), (), ()),
-    ((), (1,), (), ()),
+    ((), (3,), (), ()),
     ((), (3,), (), (3,)),
     ((), (3,), (), (3,)),
     ((1, 3), (1, 3), (1, 3), (1, 3)),
@@ -41,7 +41,7 @@ def tile_simpleconvolution_t_kernel(tc, x, weight, grad_out, out):
         keep = ctx.enter_context(tc.tile_pool(name="keep", bufs=1))
         stage = ctx.enter_context(tc.tile_pool(name="stage", bufs=8))
         quant = ctx.enter_context(tc.tile_pool(name="quant", bufs=8))
-        outs = ctx.enter_context(tc.tile_pool(name="outs", bufs=12))
+        outs = ctx.enter_context(tc.tile_pool(name="outs", bufs=13))
         psum = ctx.enter_context(tc.psum_pool(name="psum", bufs=8))
         ctx.enter_context(tc.manual_schedule())
 
@@ -92,11 +92,10 @@ def tile_simpleconvolution_t_kernel(tc, x, weight, grad_out, out):
             )
             codes_of[c] = (codes, scales)
 
-        def sweep(g, t):
-            first = sum(GROUPS[:g])
-            o = outs.tile([P, GROUPS[g] * N_TILE], F32, name="o", tag="o")
-            for k in range(GROUPS[g]):
-                codes, scales = codes_of[first + k]
+        def sweep(g, t, k0, k1):
+            o = outs.tile([P, (k1 - k0) * N_TILE], F32, name="o", tag="o")
+            for k in range(k0, k1):
+                codes, scales = codes_of[g * GROUP + k]
                 acc = psum.tile([P, N_TILE], F32, name="acc", tag="bank")
                 nc.tensor.matmul_mx(
                     out=acc[:],
@@ -107,7 +106,7 @@ def tile_simpleconvolution_t_kernel(tc, x, weight, grad_out, out):
                     start=True,
                     stop=True,
                 )
-                dst = o[:, k * N_TILE : (k + 1) * N_TILE]
+                dst = o[:, (k - k0) * N_TILE : (k - k0 + 1) * N_TILE]
                 if k in V_BANKS[g][t]:
                     late.append((dst, acc))
                 else:
@@ -119,10 +118,10 @@ def tile_simpleconvolution_t_kernel(tc, x, weight, grad_out, out):
                 nc.vector.tensor_copy(out=dst, in_=acc[:])
             late.clear()
 
-        def store(g, t, o):
-            b, px = divmod(sum(GROUPS[:g]) * N_TILE, HW)
+        def store(g, t, k0, k1, o):
+            b, px = divmod((g * GROUP + k0) * N_TILE, HW)
             out_b = out[b].rearrange("(p t) h w -> t p (h w)", t=M_TILES)
-            nc.sync.dma_start(out=out_b[t, :, px : px + GROUPS[g] * N_TILE], in_=o[:])
+            nc.sync.dma_start(out=out_b[t, :, px : px + (k1 - k0) * N_TILE], in_=o[:])
 
         w_grouped = keep.tile([P, M_TILES * P * PACK], BF16, name="w_grouped", align_bytes=64)
         w_codes = keep.tile([P, M_TILES * P], U32, name="w_codes", align_bytes=64)
@@ -156,20 +155,19 @@ def tile_simpleconvolution_t_kernel(tc, x, weight, grad_out, out):
                     prepare(done["prepared"])
                 done["prepared"] += 1
 
-        def quantise_to(c):
+        def quantise_to(c, more):
             while done["quantised"] < c:
-                prepare_to(done["quantised"] + 2)
+                prepare_to(done["quantised"] + 1 + more)
                 vector_copies_out()
                 quantise(done["quantised"])
                 done["quantised"] += 1
 
-        quantise_to(GROUPS[0])
-        for g in range(len(GROUPS)):
+        prepare_to(2)
+        quantise_to(GROUP, 0)
+        for g in range(CHUNKS // GROUP):
             for t in range(M_TILES):
-                o = sweep(g, t)
-                ahead = 0
-                if g + 1 < len(GROUPS):
-                    ahead = -(-(t + 1) * GROUPS[g + 1] // M_TILES)
-                quantise_to(sum(GROUPS[: g + 1]) + ahead)
-                vector_copies_out()
-                store(g, t, o)
+                for k0, k1 in ((0, 2), (2, 4)) if g == 0 and t == 0 else ((0, 4),):
+                    o = sweep(g, t, k0, k1)
+                    quantise_to((g + 1) * GROUP + AHEAD[g][t], 1)
+                    vector_copies_out()
+                    store(g, t, k0, k1, o)

@@ -45,9 +45,9 @@ def tile_simpleconvolution_t_kernel(tc, x, weight, grad_out, out):
         psum = ctx.enter_context(tc.psum_pool(name="psum", bufs=8))
         ctx.enter_context(tc.manual_schedule())
 
-        w_raw = keep.tile([P, M_TILES, COUT], BF16, name="w_raw")
-        b0_raw = keep.tile([P, PACK, HW], BF16, name="b0_raw")
-        b1_raw = keep.tile([P, PACK, HW], BF16, name="b1_raw")
+        w_raw = keep.tile([P, M_TILES, COUT], BF16, name="w_raw", align_bytes=256)
+        b0_raw = keep.tile([P, PACK, HW], BF16, name="b0_raw", align_bytes=256)
+        b1_raw = keep.tile([P, PACK, HW], BF16, name="b1_raw", align_bytes=256)
         raw = (b0_raw, b1_raw)
         src0 = grad_out[0].rearrange("(p j) h w -> p j (h w)", j=PACK)
         src1 = grad_out[1].rearrange("(p j) h w -> p j (h w)", j=PACK)
@@ -93,7 +93,7 @@ def tile_simpleconvolution_t_kernel(tc, x, weight, grad_out, out):
             codes_of[c] = (codes, scales)
 
         def sweep(g, t, k0, k1):
-            o = outs.tile([P, (k1 - k0) * N_TILE], F32, name="o", tag="o")
+            o = outs.tile([P, (k1 - k0) * N_TILE], F32, name="o", tag="o", align_bytes=256)
             for k in range(k0, k1):
                 codes, scales = codes_of[g * GROUP + k]
                 acc = psum.tile([P, N_TILE], F32, name="acc", tag="bank")

@@ -26,6 +26,7 @@ LO_SCALAR = (5, 6)
 HI_SCALAR = (2, 3)
 HI_LOADS = ((0, 4096),)
 GROUP = 4
+PIECES = {(0, 0): ((0, 2), (2, 4)), (3, 2): ((0, 2), (2, 4)), (3, 3): ((0, 2), (2, 3), (3, 4))}
 AHEAD = ((0, 1, 2, 4), (1, 2, 3, 4), (1, 2, 3, 4), (0, 0, 0, 0))
 V_BANKS = (
     ((), (3,), (), ()),
@@ -166,7 +167,7 @@ def tile_simpleconvolution_t_kernel(tc, x, weight, grad_out, out):
         quantise_to(GROUP, 0)
         for g in range(CHUNKS // GROUP):
             for t in range(M_TILES):
-                for k0, k1 in ((0, 2), (2, 4)) if g == 0 and t == 0 else ((0, 4),):
+                for k0, k1 in PIECES.get((g, t), ((0, GROUP),)):
                     o = sweep(g, t, k0, k1)
                     quantise_to((g + 1) * GROUP + AHEAD[g][t], 1)
                     vector_copies_out()

from contextlib import ExitStack

import concourse.mybir as mybir
from concourse.masks import make_identity

BF16 = mybir.dt.bfloat16
F32 = mybir.dt.float32
U32 = mybir.dt.uint32
U8 = mybir.dt.uint8
E4X4 = mybir.dt.float8_e4m3fn_x4
E5X4 = mybir.dt.float8_e5m2_x4

P = 128
PACK = 4
B, CIN, COUT, HW = 2, 512, 512, 4096
N_TILE = 512
M_TILES = CIN // P
CHUNKS = B * HW // N_TILE
BATCH_CHUNKS = HW // N_TILE

FLOPS = 2 * B * HW * CIN * COUT
BYTES = 2 * B * COUT * HW + 2 * CIN * COUT + 4 * B * CIN * HW

LO_VECTOR = (0, 1, 2, 3, 4)
LO_SCALAR = (5, 6)
HI_SCALAR = (2, 3)
HI_LOADS = ((0, 4096),)
GROUP = 4
PIECES = {(0, 0): ((0, 2), (2, 4)), (3, 2): ((0, 2), (2, 4)), (3, 3): ((0, 2), (2, 3), (3, 4))}
AHEAD = ((0, 1, 2, 4), (1, 2, 3, 4), (1, 2, 3, 4), (0, 0, 0, 0))
V_BANKS = (
    ((), (3,), (), ()),
    ((), (3,), (), (3,)),
    ((), (3,), (), (3,)),
    ((1, 3), (1, 3), (1, 3), (1, 3)),
)


def tile_simpleconvolution_t_kernel(tc, x, weight, grad_out, out):
    nc = tc.nc
    with ExitStack() as ctx:
        keep = ctx.enter_context(tc.tile_pool(name="keep", bufs=1))
        stage = ctx.enter_context(tc.tile_pool(name="stage", bufs=8))
        quant = ctx.enter_context(tc.tile_pool(name="quant", bufs=8))
        outs = ctx.enter_context(tc.tile_pool(name="outs", bufs=13))
        psum = ctx.enter_context(tc.psum_pool(name="psum", bufs=8))
        ctx.enter_context(tc.manual_schedule())

        w_raw = keep.tile([P, M_TILES, COUT], BF16, name="w_raw", align_bytes=256)
        b0_raw = keep.tile([P, PACK, HW], BF16, name="b0_raw", align_bytes=256)
        b1_raw = keep.tile([P, PACK, HW], BF16, name="b1_raw", align_bytes=256)
        raw = (b0_raw, b1_raw)
        src0 = grad_out[0].rearrange("(p j) h w -> p j (h w)", j=PACK)
        src1 = grad_out[1].rearrange("(p j) h w -> p j (h w)", j=PACK)
        nc.sync.dma_start(out=w_raw[:], in_=weight.rearrange("(p t) k -> p t k", t=M_TILES))
        nc.sync.dma_start(out=b0_raw[:, 0:2, :], in_=src0[:, 0:2, :])
        for px0, npx in HI_LOADS:
            nc.sync.dma_start(out=b0_raw[:, 2:4, px0 : px0 + npx], in_=src0[:, 2:4, px0 : px0 + npx])
        nc.sync.dma_start(out=b1_raw[:], in_=src1)

        ident = keep.tile([P, P], F32, name="ident")
        make_identity(nc, ident[:])

        grouped_of = {}
        codes_of = {}
        late = []

        def regroup(c, j0, j1, on_scalar):
            if c not in grouped_of:
                grouped = stage.tile([P, N_TILE, PACK], BF16, name="grouped", tag="grouped", align_bytes=64)
                grouped_of[c] = grouped
            b, k = divmod(c, BATCH_CHUNKS)
            dst = grouped_of[c][:].rearrange("p (c i) j -> p c j i", i=4)[:, :, j0:j1, :]
            src = raw[b][:, j0:j1, k * N_TILE : (k + 1) * N_TILE].rearrange("p j (c i) -> p c j i", i=4)
            if on_scalar:
                nc.scalar.copy(out=dst, in_=src)
            else:
                nc.vector.tensor_copy(out=dst, in_=src)

        def prepare(c):
            if c in LO_VECTOR or c in LO_SCALAR:
                regroup(c, 2, PACK, c in HI_SCALAR)
            else:
                regroup(c, 0, PACK, False)

        def quantise(c):
            codes = quant.tile([P, N_TILE], U32, name="codes", tag="codes", align_bytes=64)
            scales = quant.tile([P, N_TILE], U8, name="scales", tag="scales", align_bytes=64)
            nc.vector.quantize_mx(
                out=codes[:].bitcast(E5X4),
                scales=scales[:],
                in_=grouped_of[c][:].rearrange("p w j -> p (w j)"),
            )
            codes_of[c] = (codes, scales)

        def sweep(g, t, k0, k1):
            o = outs.tile([P, (k1 - k0) * N_TILE], F32, name="o", tag="o", align_bytes=256)
            for k in range(k0, k1):
                codes, scales = codes_of[g * GROUP + k]
                acc = psum.tile([P, N_TILE], F32, name="acc", tag="bank")
                nc.tensor.matmul_mx(
                    out=acc[:],
                    lhsT=w_codes[:, t * P : (t + 1) * P].bitcast(E4X4),
                    lhsT_scale=w_scales[:, t * P : (t + 1) * P],
                    rhs=codes[:].bitcast(E5X4),
                    rhs_scale=scales[:],
                    start=True,
                    stop=True,
                )
                dst = o[:, (k - k0) * N_TILE : (k - k0 + 1) * N_TILE]
                if k in V_BANKS[g][t]:
                    late.append((dst, acc))
                else:
                    nc.scalar.copy(out=dst, in_=acc[:])
            return o

        def vector_copies_out():
            for dst, acc in late:
                nc.vector.tensor_copy(out=dst, in_=acc[:])
            late.clear()

        def store(g, t, k0, k1, o):
            b, px = divmod((g * GROUP + k0) * N_TILE, HW)
            out_b = out[b].rearrange("(p t) h w -> t p (h w)", t=M_TILES)
            nc.sync.dma_start(out=out_b[t, :, px : px + (k1 - k0) * N_TILE], in_=o[:])

        w_grouped = keep.tile([P, M_TILES * P * PACK], BF16, name="w_grouped", align_bytes=64)
        w_codes = keep.tile([P, M_TILES * P], U32, name="w_codes", align_bytes=64)
        w_scales = keep.tile([P, M_TILES * P], U8, name="w_scales", align_bytes=64)
        w_words = w_raw[:].bitcast(F32).rearrange("p t (q u) -> p t u q", u=2)
        w_grouped_words = w_grouped[:].bitcast(F32).rearrange("p (t i u) -> p t i u", t=M_TILES, u=2)
        for half in range(2):
            bank = psum.tile([P, N_TILE], F32, name="bank", tag="bank")
            planes = bank[:].rearrange("p (t u i) -> p t u i", t=2, u=2)
            for tt in range(2):
                for u in range(2):
                    nc.tensor.transpose(planes[:, tt, u, :], w_words[:, 2 * half + tt, u, :], ident[:])
            nc.scalar.copy(
                out=w_grouped_words[:, 2 * half : 2 * half + 2, :, :],
                in_=planes.rearrange("p t u i -> p t i u"),
            )
        nc.vector.quantize_mx(out=w_codes[:].bitcast(E4X4), scales=w_scales[:], in_=w_grouped[:])

        for c in LO_SCALAR:
            regroup(c, 0, 2, True)
        for c in LO_VECTOR:
            regroup(c, 0, 2, False)
        for c in HI_SCALAR:
            prepare(c)

        done = {"prepared": 0, "quantised": 0}

        def prepare_to(c):
            while done["prepared"] < min(c, CHUNKS):
                if done["prepared"] not in HI_SCALAR:
                    prepare(done["prepared"])
                done["prepared"] += 1

        def quantise_to(c, more):
            while done["quantised"] < c:
                prepare_to(done["quantised"] + 1 + more)
                vector_copies_out()
                quantise(done["quantised"])
                done["quantised"] += 1

        prepare_to(2)
        quantise_to(GROUP, 0)
        for g in range(CHUNKS // GROUP):
            for t in range(M_TILES):
                for k0, k1 in PIECES.get((g, t), ((0, GROUP),)):
                    o = sweep(g, t, k0, k1)
                    quantise_to((g + 1) * GROUP + AHEAD[g][t], 1)
                    vector_copies_out()
                    store(g, t, k0, k1, o)
